import numpy as np
import ml_dtypes


def mxq(x, axis, fmt="e4m3"):
    dtype, down = {"e4m3": (ml_dtypes.float8_e4m3fn, 7), "e5m2": (ml_dtypes.float8_e5m2, 14)}[fmt]
    v = np.moveaxis(np.asarray(x, np.float32).astype(ml_dtypes.bfloat16).astype(np.float64), axis, -1)
    blocks = v.reshape(v.shape[:-1] + (-1, 32))
    amax = np.abs(blocks).max(-1, keepdims=True)
    byte = np.maximum(np.where(amax > 0, np.frexp(amax)[1] - 1 + 127, 0) - down, 1)
    scale = np.exp2(byte - 127.0)
    codes = (blocks / scale).astype(np.float32).astype(dtype).astype(np.float64)
    return np.moveaxis((codes * scale).reshape(v.shape), -1, axis)


WIDE = False


def mx_kscale(k):
    if not WIDE:
        return np.ones(k)
    levels = np.array([10, -10, 5, -5, 0])
    a = np.random.permutation(np.resize(levels, k // 512 * 4)).reshape(k // 512, 4)
    idx = np.arange(k)
    return np.exp2(a[idx // 512, idx % 128 // 32])


BF16 = ml_dtypes.bfloat16


def bf(x):
    return np.asarray(x, np.float32).astype(BF16)


def f64(x):
    return np.asarray(x).astype(np.float64)


E2M1 = np.array([0.0, 0.5, 1.0, 1.5, 2.0, 3.0, 4.0, 6.0, -0.0, -0.5, -1.0, -1.5, -2.0, -3.0, -4.0, -6.0])


def pack_weight(w, fmt):
    k, n = w.shape
    w = f64(bf(w)).reshape(k // 32, 32, n)
    amax = np.abs(w).max(1)
    if fmt == "e4m3":
        byte = np.frexp(amax)[1] - 1 + 127 - 7
    else:
        mant, ex = np.frexp(amax / 6.0)
        byte = np.where(mant > 0.5, ex, ex - 1) + 127
    byte = np.clip(np.where(amax > 0, byte, 1), 1, 254)
    scaled = (w * np.exp2(127.0 - byte)[:, None, :]).reshape(k, n).astype(np.float32)
    by_word = np.ascontiguousarray(scaled.reshape(k // 512, 128, 4, n).transpose(0, 1, 3, 2))
    if fmt == "e4m3":
        words = by_word.astype(ml_dtypes.float8_e4m3fn).view(np.uint8)
    else:
        c = by_word.astype(ml_dtypes.float4_e2m1fn).view(np.uint8) & 0xF
        words = c[..., 0::2] | (c[..., 1::2] << 4)
    return np.ascontiguousarray(words), np.ascontiguousarray(byte.astype(np.uint8).reshape(k // 512, 16, n))


def unpack_weight(words, scales, fmt):
    g, p, n, _ = words.shape
    if fmt == "e4m3":
        vals = np.ascontiguousarray(words).view(ml_dtypes.float8_e4m3fn).astype(np.float64)
    else:
        nib = np.empty((g, p, n, 4), np.uint8)
        nib[..., 0::2] = words & 0xF
        nib[..., 1::2] = words >> 4
        vals = E2M1[nib]
    vals = vals * np.repeat(np.exp2(scales.astype(np.float64) - 127.0), 8, axis=1)[..., None]
    return vals.transpose(0, 1, 3, 2).reshape(g * 512, n)


B, P, L, FI, FO = 128, 2, 3, 512, 512
C = (L + 1) * (L + 1)
D = L + 1


def setup_inputs():
    s = mx_kscale(FI)
    x = bf(np.random.standard_normal((B, P, C, FI)) * s)
    we = np.random.standard_normal((L + 1, FI, FO)) / np.sqrt(FI) / s[:, None]
    wo = np.random.standard_normal((L + 1, FI, FO)) / np.sqrt(FI) / s[:, None]
    b = bf(np.random.standard_normal(FO) * 0.5)
    we_words, we_scales = pack_weight(we.reshape(-1, FO), "e4m3")
    wo_words, wo_scales = pack_weight(wo.reshape(-1, FO), "e4m3")
    return {"x": x,
            "W_e_words": we_words, "W_e_scales": we_scales,
            "W_o_words": wo_words, "W_o_scales": wo_scales,
            "b": b}


def reference(x, W_e_words, W_e_scales, W_o_words, W_o_scales, b):
    xq = mxq(f64(x), 3, "e4m3")
    weq = unpack_weight(W_e_words, W_e_scales, "e4m3").reshape(D, FI, FO)
    woq = unpack_weight(W_o_words, W_o_scales, "e4m3").reshape(D, FI, FO)
    outs_e, outs_o = [], []
    for l in range(L + 1):
        seg = xq[:, :, l * l:(l + 1) * (l + 1), :]
        oe = seg[:, 0] @ weq[l]
        if l == 0:
            oe = oe + f64(b)
        oo = seg[:, 1] @ woq[l]
        outs_e.append(oe)
        outs_o.append(oo)
    return np.stack([np.concatenate(outs_e, axis=-2), np.concatenate(outs_o, axis=-2)], axis=-3)

@@ -1,0 +1,149 @@
+from contextlib import ExitStack
+
+import concourse.mybir as mybir
+from concourse.masks import make_identity
+
+BF16 = mybir.dt.bfloat16
+F32 = mybir.dt.float32
+I32 = mybir.dt.int32
+U32 = mybir.dt.uint32
+U8 = mybir.dt.uint8
+FP8X4 = mybir.dt.float8_e4m3fn_x4
+
+P = 128
+ITEMS = 128
+PARITIES = 2
+COMPONENTS = 16
+DEGREES = 4
+F_IN = 512
+F_OUT = 512
+PACK = 4
+PAIRS = 2
+DEGREE_OF = [l for l in range(DEGREES) for m in range(2 * l + 1)]
+
+GROUP = 4
+GROUPS = PARITIES * COMPONENTS // GROUP
+BANK_SLABS = 2
+LOAD_GROUPS = 2
+LOADS = GROUPS // LOAD_GROUPS
+AHEAD = 2
+
+FLOPS = 2 * ITEMS * PARITIES * COMPONENTS * F_IN * F_OUT
+
+
+def tile_dense_pa_e_kernel(tc, x, W_e_words, W_e_scales, W_o_words, W_o_scales, b, out):
+    nc = tc.nc
+    given_words = [W_e_words, W_o_words]
+    given_scales = [W_e_scales, W_o_scales]
+
+    with ExitStack() as ctx:
+        keep = ctx.enter_context(tc.tile_pool(name="keep", bufs=1))
+        x_pool = ctx.enter_context(tc.tile_pool(name="x_pool", bufs=LOADS))
+        stage = ctx.enter_context(tc.tile_pool(name="stage", bufs=AHEAD + 1))
+        results = ctx.enter_context(tc.tile_pool(name="results", bufs=GROUPS))
+        turned_pool = ctx.enter_context(tc.psum_pool(name="turned_pool", bufs=AHEAD * GROUP // BANK_SLABS))
+        acc_pool = ctx.enter_context(tc.psum_pool(name="acc_pool", bufs=GROUP))
+        ctx.enter_context(tc.manual_schedule())
+
+        w_planes = keep.tile([P, PARITIES, F_OUT], U8, align_bytes=64)
+        nc.vector.memset(w_planes[:].bitcast(I32), 0)
+        bias_row = keep.tile([P, F_OUT], BF16)
+        nc.vector.memset(bias_row[:], 0.0)
+        ones = keep.tile([P, P], BF16)
+        nc.vector.memset(ones[:], 1.0)
+        identity = keep.tile([P, P], F32)
+        make_identity(nc, identity[:])
+        nc.scalar.dma_start(out=bias_row[0:1, :], in_=b.unsqueeze(0))
+
+        x_tiles = [x_pool.tile([P, LOAD_GROUPS * GROUP, F_IN], BF16, name="x_tile") for i in range(LOADS)]
+        w_words = [keep.tile([P, DEGREES, F_OUT], U32, name="w_words%d" % parity, align_bytes=64) for parity in range(PARITIES)]
+
+        def load_x(i):
+            comps = LOAD_GROUPS * GROUP
+            parity, first = divmod(i * comps, COMPONENTS)
+            nc.sync.dma_start(out=x_tiles[i][:], in_=x[:, parity, first : first + comps, :])
+
+        def load_weights(parity):
+            for quadrant in range(4):
+                nc.sync.dma_start(
+                    out=w_planes[32 * quadrant : 32 * quadrant + 16, parity, :].bitcast(I32),
+                    in_=given_scales[parity][:, 4 * quadrant : 4 * quadrant + 4, :].bitcast(I32),
+                )
+            nc.sync.dma_start(
+                out=w_words[parity][:].bitcast(I32),
+                in_=given_words[parity].rearrange("g p n t -> p g (n t)").bitcast(I32),
+            )
+
+        for parity in range(PARITIES):
+            load_x(2 * parity)
+            load_x(2 * parity + 1)
+            load_weights(parity)
+
+        turned = {}
+        grouped = {}
+        x_codes = {}
+        x_planes = {}
+
+        def transpose_group(j):
+            words = x_tiles[j // LOAD_GROUPS][:].bitcast(F32)
+            for half in range(GROUP // BANK_SLABS):
+                bank = turned_pool.tile([P, BANK_SLABS, PAIRS, ITEMS], F32, name="turned")
+                turned[(j, half)] = bank
+                for s in range(BANK_SLABS):
+                    comp = (j % LOAD_GROUPS) * GROUP + half * BANK_SLABS + s
+                    for u in range(PAIRS):
+                        nc.tensor.transpose(bank[:, s, u, :], words[:, comp, u : F_IN // 2 : PAIRS], identity[:])
+
+        def regroup(j):
+            grouped[j] = stage.tile([P, GROUP * ITEMS * PACK], BF16, name="grouped", align_bytes=64)
+            by_item = grouped[j][:].bitcast(F32).rearrange("p (s n u) -> p s n u", n=ITEMS, u=PAIRS)
+            for half in range(GROUP // BANK_SLABS):
+                nc.vector.tensor_copy(
+                    out=by_item[:, half * BANK_SLABS : (half + 1) * BANK_SLABS, :, :],
+                    in_=turned[(j, half)][:].rearrange("p s u n -> p s n u"),
+                )
+
+        def quantise(j):
+            x_codes[j] = stage.tile([P, GROUP * ITEMS], U32, name="x_codes", align_bytes=64)
+            x_planes[j] = stage.tile([P, GROUP * ITEMS], U8, name="x_planes", align_bytes=64)
+            nc.vector.quantize_mx(out=x_codes[j][:].bitcast(FP8X4), scales=x_planes[j][:], in_=grouped[j][:])
+
+        def multiply_and_store(j):
+            parity, first = divmod(j * GROUP, COMPONENTS)
+            result = results.tile([P, GROUP, F_OUT], F32, name="result")
+            for s in range(GROUP):
+                degree = DEGREE_OF[first + s]
+                items = slice(s * ITEMS, (s + 1) * ITEMS)
+                acc = acc_pool.tile([P, F_OUT], F32, name="acc")
+                nc.tensor.matmul_mx(
+                    out=acc[:],
+                    lhsT=x_codes[j][:, items].bitcast(FP8X4),
+                    lhsT_scale=x_planes[j][:, items],
+                    rhs=w_words[parity][:, degree, :].bitcast(FP8X4),
+                    rhs_scale=w_planes[4 * degree : P, parity, :],
+                    start=True,
+                    stop=True,
+                )
+                if parity == 0 and first + s == 0:
+                    nc.vector.tensor_tensor(out=result[:, s, :], in0=acc[:], in1=bias_all[:], op=mybir.AluOpType.add)
+                else:
+                    nc.scalar.copy(out=result[:, s, :], in_=acc[:])
+            nc.sync.dma_start(out=out[:, parity, first : first + GROUP, :], in_=result[:])
+
+        for j in range(AHEAD):
+            transpose_group(j)
+        bias_bank = acc_pool.tile([P, F_OUT], F32, name="acc")
+        nc.tensor.matmul(out=bias_bank[:], lhsT=ones[:], rhs=bias_row[:], start=True, stop=True)
+        bias_all = keep.tile([P, F_OUT], F32)
+        nc.scalar.copy(out=bias_all[:], in_=bias_bank[:])
+        for j in range(AHEAD):
+            regroup(j)
+        quantise(0)
+        for j in range(GROUPS):
+            if j + AHEAD < GROUPS:
+                transpose_group(j + AHEAD)
+            multiply_and_store(j)
+            if j + AHEAD < GROUPS:
+                regroup(j + AHEAD)
+            if j + 1 < GROUPS:
+                quantise(j + 1)

@@ -74,15 +74,19 @@ def tile_dense_pa_e_kernel(tc, x, W_e_words, W_e_scales, W_o_words, W_o_scales, 
                 in_=given_words[parity].rearrange("g p n t -> p g (n t)").bitcast(I32),
             )
 
-        for parity in range(PARITIES):
-            load_x(2 * parity)
-            load_x(2 * parity + 1)
-            load_weights(parity)
+        load_x(0)
+        load_weights(0)
+        load_x(1)
+        load_x(2)
+        load_weights(1)
+        load_x(3)
 
         turned = {}
         grouped = {}
         x_codes = {}
         x_planes = {}
+        left_to_vector = []
+        to_store = []
 
         def transpose_group(j):
             words = x_tiles[j // LOAD_GROUPS][:].bitcast(F32)
@@ -126,9 +130,19 @@ def tile_dense_pa_e_kernel(tc, x, W_e_words, W_e_scales, W_o_words, W_o_scales, 
                 )
                 if parity == 0 and first + s == 0:
                     nc.vector.tensor_tensor(out=result[:, s, :], in0=acc[:], in1=bias_all[:], op=mybir.AluOpType.add)
+                elif j % 2 == 1 and s == GROUP - 1:
+                    left_to_vector.append((result[:, s, :], acc))
                 else:
                     nc.scalar.copy(out=result[:, s, :], in_=acc[:])
-            nc.sync.dma_start(out=out[:, parity, first : first + GROUP, :], in_=result[:])
+            to_store.append((out[:, parity, first : first + GROUP, :], result))
+
+        def finish_group():
+            for target, acc in left_to_vector:
+                nc.vector.tensor_copy(out=target, in_=acc[:])
+            left_to_vector.clear()
+            for target, result in to_store:
+                nc.sync.dma_start(out=target, in_=result[:])
+            to_store.clear()
 
         for j in range(AHEAD):
             transpose_group(j)
@@ -140,10 +154,14 @@ def tile_dense_pa_e_kernel(tc, x, W_e_words, W_e_scales, W_o_words, W_o_scales, 
             regroup(j)
         quantise(0)
         for j in range(GROUPS):
+            if j == 0:
+                multiply_and_store(j)
             if j + AHEAD < GROUPS:
                 transpose_group(j + AHEAD)
-            multiply_and_store(j)
+            if j > 0:
+                multiply_and_store(j)
             if j + AHEAD < GROUPS:
                 regroup(j + AHEAD)
             if j + 1 < GROUPS:
                 quantise(j + 1)
+            finish_group()

@@ -45,7 +45,7 @@ def tile_dense_pa_e_kernel(tc, x, W_e_words, W_e_scales, W_o_words, W_o_scales, 
         acc_pool = ctx.enter_context(tc.psum_pool(name="acc_pool", bufs=GROUP))
         ctx.enter_context(tc.manual_schedule())
 
-        w_planes = keep.tile([P, PARITIES, F_OUT], U8, align_bytes=64)
+        w_planes = keep.tile([P, PARITIES, F_OUT], U8, align_bytes=256)
         nc.vector.memset(w_planes[:].bitcast(I32), 0)
         bias_row = keep.tile([P, F_OUT], BF16)
         nc.vector.memset(bias_row[:], 0.0)
@@ -55,8 +55,8 @@ def tile_dense_pa_e_kernel(tc, x, W_e_words, W_e_scales, W_o_words, W_o_scales, 
         make_identity(nc, identity[:])
         nc.scalar.dma_start(out=bias_row[0:1, :], in_=b.unsqueeze(0))
 
-        x_tiles = [x_pool.tile([P, LOAD_GROUPS * GROUP, F_IN], BF16, name="x_tile") for i in range(LOADS)]
-        w_words = [keep.tile([P, DEGREES, F_OUT], U32, name="w_words%d" % parity, align_bytes=64) for parity in range(PARITIES)]
+        x_tiles = [x_pool.tile([P, LOAD_GROUPS * GROUP, F_IN], BF16, name="x_tile", align_bytes=256) for i in range(LOADS)]
+        w_words = [keep.tile([P, DEGREES, F_OUT], U32, name="w_words%d" % parity, align_bytes=256) for parity in range(PARITIES)]
 
         def load_x(i):
             comps = LOAD_GROUPS * GROUP
@@ -114,7 +114,7 @@ def tile_dense_pa_e_kernel(tc, x, W_e_words, W_e_scales, W_o_words, W_o_scales, 
 
         def multiply_and_store(j):
             parity, first = divmod(j * GROUP, COMPONENTS)
-            result = results.tile([P, GROUP, F_OUT], F32, name="result")
+            result = results.tile([P, GROUP, F_OUT], F32, name="result", align_bytes=256)
             for s in range(GROUP):
                 degree = DEGREE_OF[first + s]
                 items = slice(s * ITEMS, (s + 1) * ITEMS)

@@ -45,7 +45,7 @@ def tile_dense_pa_e_kernel(tc, x, W_e_words, W_e_scales, W_o_words, W_o_scales, 
         acc_pool = ctx.enter_context(tc.psum_pool(name="acc_pool", bufs=GROUP))
         ctx.enter_context(tc.manual_schedule())
 
-        w_planes = keep.tile([P, PARITIES, F_OUT], U8, align_bytes=256)
+        w_planes = keep.tile([P, PARITIES, F_OUT], U8, align_bytes=64)
         nc.vector.memset(w_planes[:].bitcast(I32), 0)
         bias_row = keep.tile([P, F_OUT], BF16)
         nc.vector.memset(bias_row[:], 0.0)
@@ -56,7 +56,7 @@ def tile_dense_pa_e_kernel(tc, x, W_e_words, W_e_scales, W_o_words, W_o_scales, 
         nc.scalar.dma_start(out=bias_row[0:1, :], in_=b.unsqueeze(0))
 
         x_tiles = [x_pool.tile([P, LOAD_GROUPS * GROUP, F_IN], BF16, name="x_tile", align_bytes=256) for i in range(LOADS)]
-        w_words = [keep.tile([P, DEGREES, F_OUT], U32, name="w_words%d" % parity, align_bytes=256) for parity in range(PARITIES)]
+        w_words = [keep.tile([P, DEGREES, F_OUT], U32, name="w_words%d" % parity, align_bytes=64) for parity in range(PARITIES)]
 
         def load_x(i):
             comps = LOAD_GROUPS * GROUP

from contextlib import ExitStack

import concourse.mybir as mybir
from concourse.masks import make_identity

BF16 = mybir.dt.bfloat16
F32 = mybir.dt.float32
I32 = mybir.dt.int32
U32 = mybir.dt.uint32
U8 = mybir.dt.uint8
FP8X4 = mybir.dt.float8_e4m3fn_x4

P = 128
ITEMS = 128
PARITIES = 2
COMPONENTS = 16
DEGREES = 4
F_IN = 512
F_OUT = 512
PACK = 4
PAIRS = 2
DEGREE_OF = [l for l in range(DEGREES) for m in range(2 * l + 1)]

GROUP = 4
GROUPS = PARITIES * COMPONENTS // GROUP
BANK_SLABS = 2
LOAD_GROUPS = 2
LOADS = GROUPS // LOAD_GROUPS
AHEAD = 2

FLOPS = 2 * ITEMS * PARITIES * COMPONENTS * F_IN * F_OUT


def tile_dense_pa_e_kernel(tc, x, W_e_words, W_e_scales, W_o_words, W_o_scales, b, out):
    nc = tc.nc
    given_words = [W_e_words, W_o_words]
    given_scales = [W_e_scales, W_o_scales]

    with ExitStack() as ctx:
        keep = ctx.enter_context(tc.tile_pool(name="keep", bufs=1))
        x_pool = ctx.enter_context(tc.tile_pool(name="x_pool", bufs=LOADS))
        stage = ctx.enter_context(tc.tile_pool(name="stage", bufs=AHEAD + 1))
        results = ctx.enter_context(tc.tile_pool(name="results", bufs=GROUPS))
        turned_pool = ctx.enter_context(tc.psum_pool(name="turned_pool", bufs=AHEAD * GROUP // BANK_SLABS))
        acc_pool = ctx.enter_context(tc.psum_pool(name="acc_pool", bufs=GROUP))
        ctx.enter_context(tc.manual_schedule())

        w_planes = keep.tile([P, PARITIES, F_OUT], U8, align_bytes=64)
        nc.vector.memset(w_planes[:].bitcast(I32), 0)
        bias_row = keep.tile([P, F_OUT], BF16)
        nc.vector.memset(bias_row[:], 0.0)
        ones = keep.tile([P, P], BF16)
        nc.vector.memset(ones[:], 1.0)
        identity = keep.tile([P, P], F32)
        make_identity(nc, identity[:])
        nc.scalar.dma_start(out=bias_row[0:1, :], in_=b.unsqueeze(0))

        x_tiles = [x_pool.tile([P, LOAD_GROUPS * GROUP, F_IN], BF16, name="x_tile", align_bytes=256) for i in range(LOADS)]
        w_words = [keep.tile([P, DEGREES, F_OUT], U32, name="w_words%d" % parity, align_bytes=64) for parity in range(PARITIES)]

        def load_x(i):
            comps = LOAD_GROUPS * GROUP
            parity, first = divmod(i * comps, COMPONENTS)
            nc.sync.dma_start(out=x_tiles[i][:], in_=x[:, parity, first : first + comps, :])

        def load_weights(parity):
            for quadrant in range(4):
                nc.sync.dma_start(
                    out=w_planes[32 * quadrant : 32 * quadrant + 16, parity, :].bitcast(I32),
                    in_=given_scales[parity][:, 4 * quadrant : 4 * quadrant + 4, :].bitcast(I32),
                )
            nc.sync.dma_start(
                out=w_words[parity][:].bitcast(I32),
                in_=given_words[parity].rearrange("g p n t -> p g (n t)").bitcast(I32),
            )

        load_x(0)
        load_weights(0)
        load_x(1)
        load_x(2)
        load_weights(1)
        load_x(3)

        turned = {}
        grouped = {}
        x_codes = {}
        x_planes = {}
        left_to_vector = []
        to_store = []

        def transpose_group(j):
            words = x_tiles[j // LOAD_GROUPS][:].bitcast(F32)
            for half in range(GROUP // BANK_SLABS):
                bank = turned_pool.tile([P, BANK_SLABS, PAIRS, ITEMS], F32, name="turned")
                turned[(j, half)] = bank
                for s in range(BANK_SLABS):
                    comp = (j % LOAD_GROUPS) * GROUP + half * BANK_SLABS + s
                    for u in range(PAIRS):
                        nc.tensor.transpose(bank[:, s, u, :], words[:, comp, u : F_IN // 2 : PAIRS], identity[:])

        def regroup(j):
            grouped[j] = stage.tile([P, GROUP * ITEMS * PACK], BF16, name="grouped", align_bytes=64)
            by_item = grouped[j][:].bitcast(F32).rearrange("p (s n u) -> p s n u", n=ITEMS, u=PAIRS)
            for half in range(GROUP // BANK_SLABS):
                nc.vector.tensor_copy(
                    out=by_item[:, half * BANK_SLABS : (half + 1) * BANK_SLABS, :, :],
                    in_=turned[(j, half)][:].rearrange("p s u n -> p s n u"),
                )

        def quantise(j):
            x_codes[j] = stage.tile([P, GROUP * ITEMS], U32, name="x_codes", align_bytes=64)
            x_planes[j] = stage.tile([P, GROUP * ITEMS], U8, name="x_planes", align_bytes=64)
            nc.vector.quantize_mx(out=x_codes[j][:].bitcast(FP8X4), scales=x_planes[j][:], in_=grouped[j][:])

        def multiply_and_store(j):
            parity, first = divmod(j * GROUP, COMPONENTS)
            result = results.tile([P, GROUP, F_OUT], F32, name="result", align_bytes=256)
            for s in range(GROUP):
                degree = DEGREE_OF[first + s]
                items = slice(s * ITEMS, (s + 1) * ITEMS)
                acc = acc_pool.tile([P, F_OUT], F32, name="acc")
                nc.tensor.matmul_mx(
                    out=acc[:],
                    lhsT=x_codes[j][:, items].bitcast(FP8X4),
                    lhsT_scale=x_planes[j][:, items],
                    rhs=w_words[parity][:, degree, :].bitcast(FP8X4),
                    rhs_scale=w_planes[4 * degree : P, parity, :],
                    start=True,
                    stop=True,
                )
                if parity == 0 and first + s == 0:
                    nc.vector.tensor_tensor(out=result[:, s, :], in0=acc[:], in1=bias_all[:], op=mybir.AluOpType.add)
                elif j % 2 == 1 and s == GROUP - 1:
                    left_to_vector.append((result[:, s, :], acc))
                else:
                    nc.scalar.copy(out=result[:, s, :], in_=acc[:])
            to_store.append((out[:, parity, first : first + GROUP, :], result))

        def finish_group():
            for target, acc in left_to_vector:
                nc.vector.tensor_copy(out=target, in_=acc[:])
            left_to_vector.clear()
            for target, result in to_store:
                nc.sync.dma_start(out=target, in_=result[:])
            to_store.clear()

        for j in range(AHEAD):
            transpose_group(j)
        bias_bank = acc_pool.tile([P, F_OUT], F32, name="acc")
        nc.tensor.matmul(out=bias_bank[:], lhsT=ones[:], rhs=bias_row[:], start=True, stop=True)
        bias_all = keep.tile([P, F_OUT], F32)
        nc.scalar.copy(out=bias_all[:], in_=bias_bank[:])
        for j in range(AHEAD):
            regroup(j)
        quantise(0)
        for j in range(GROUPS):
            if j == 0:
                multiply_and_store(j)
            if j + AHEAD < GROUPS:
                transpose_group(j + AHEAD)
            if j > 0:
                multiply_and_store(j)
            if j + AHEAD < GROUPS:
                regroup(j + AHEAD)
            if j + 1 < GROUPS:
                quantise(j + 1)
            finish_group()
